import numpy as np
import ml_dtypes

BF16 = ml_dtypes.bfloat16


def bf(x):
    return np.asarray(x, np.float32).astype(BF16)


def f32(x):
    return np.asarray(x, np.float32)


def f64(x):
    return np.asarray(x).astype(np.float64)


def striped(idx):
    return np.tile(idx.reshape(-1, 16).T, (8, 1))


D, S, N, E, R, ERF_TERMS = 128, 2048, 256, 5, 4, 150
ERF_LIM = 6.0


def erf(a):
    c = np.clip(a, -ERF_LIM, ERF_LIM)
    term = c.copy()
    total = c.copy()
    for n in range(1, ERF_TERMS):
        term = term * 2.0 * c * c / (2.0 * n + 1.0)
        total = total + term
    val = 2.0 / np.sqrt(np.pi) * np.exp(-c * c) * total
    return np.where(np.abs(a) > ERF_LIM, np.sign(a), val)


def gelu_erf(v):
    return 0.5 * v * (1.0 + erf(v / np.sqrt(2.0)))


def sigmoid(v):
    return 1.0 / (1.0 + np.exp(-v))


def setup_inputs():
    return {"ent": f32(bf(2.0 * np.random.standard_normal((E * D, S)))), "rot": f32(np.random.standard_normal((R * D, N))), "boost": f32(1.0 + np.random.standard_normal((R * D, N))), "offs": striped(np.random.permutation(np.tile(np.arange(S), 2))[:N])}


def reference(ent, rot, boost, offs):
    idx = offs[:16].T.reshape(-1)
    l0, l1, l2, l3, l4 = f64(ent).reshape(E, D, S)[:, :, idx]
    q0, q1, q2, q3 = gelu_erf(f64(rot)).reshape(R, D, N)
    s0 = l1 * q0 - l2 * q1 - l3 * q2 - l4 * q3
    s1 = l1 * q1 + q0 * l2 + l3 * q3 - q2 * l4
    s2 = l1 * q2 + q0 * l3 + l4 * q1 - q3 * l2
    s3 = l1 * q3 + q0 * l4 + l2 * q2 - q1 * l3
    s = np.stack([s0, s1, s2, s3])
    b = sigmoid(f64(boost)).reshape(R, D, N) / 4.0
    b2 = (b * b).sum(axis=0)
    bb = np.sqrt(np.eye(R)[:, :, None, None] + b[:, None] * b[None, :])
    xt = l0 * b2 + (b * s).sum(axis=0)
    xs = l0[None] * b + (bb * s[None]).sum(axis=1)
    x = np.concatenate([-xt[None], xs]).reshape(E * D, N)
    return 2.0 + 2.0 * (f64(ent).T @ x) / D

@@ -1,0 +1,128 @@
+import concourse.mybir as mybir
+
+F32 = mybir.dt.float32
+BF16 = mybir.dt.bfloat16
+U16 = mybir.dt.uint16
+ALU = mybir.AluOpType
+FN = mybir.ActivationFunctionType
+
+P = 128
+S = 2048
+N = 256
+E = 5
+R = 4
+
+FLOPS = 2 * E * P * S * N
+
+ROTATION = {
+    1: ((0, 1), (1, 1), (2, 1), (3, 1)),
+    2: ((1, -1), (0, 1), (3, -1), (2, 1)),
+    3: ((2, -1), (3, 1), (0, 1), (1, -1)),
+    4: ((3, -1), (2, -1), (1, 1), (0, 1)),
+}
+
+SMALLEST_B = 1e-30
+
+
+def tile_lorentzkg_kernel(tc, ent, rot, boost, offs, out):
+    nc = tc.nc
+    with (
+        tc.tile_pool(name="held", bufs=1) as held,
+        tc.tile_pool(name="terms", bufs=4) as terms,
+        tc.tile_pool(name="staging", bufs=4) as staging,
+        tc.psum_pool(name="banks", bufs=4) as banks,
+    ):
+        offsets = held.tile([P, N // 16], U16, name="offsets")
+        nc.sync.dma_start(offsets[:], offs)
+        rot_in = held.tile([P, R, N], F32, name="rot_in")
+        nc.scalar.dma_start(rot_in[:], rot.rearrange("(m p) j -> p m j", p=P))
+        boost_in = held.tile([P, R, N], F32, name="boost_in")
+        nc.scalar.dma_start(boost_in[:], boost.rearrange("(m p) j -> p m j", p=P))
+        table = [held.tile([P, S], F32, name=f"table{m}") for m in range(E)]
+        for m in (1, 2, 3, 4, 0):
+            nc.sync.dma_start(table[m][:], ent[m * P : (m + 1) * P, :])
+
+        def add_components(total, parts, halves):
+            nc.vector.tensor_tensor(halves[:], parts[:, 0:2, :], parts[:, 2:4, :], ALU.add)
+            nc.vector.tensor_tensor(total, halves[:, 0, :], halves[:, 1, :], ALU.add)
+
+        q = held.tile([P, R, N], F32, name="q")
+        nc.scalar.activation(q[:], rot_in[:], FN.Gelu)
+        sigmoid = held.tile([P, R, N], F32, name="sigmoid")
+        nc.scalar.activation(sigmoid[:], boost_in[:], FN.Sigmoid)
+        b = held.tile([P, R, N], F32, name="b")
+        nc.vector.tensor_scalar(b[:], sigmoid[:], 0.25, SMALLEST_B, ALU.mult, ALU.max)
+        b_squared = held.tile([P, R, N], F32, name="b_squared")
+        nc.vector.tensor_tensor(b_squared[:], b[:], b[:], ALU.mult)
+        b_squared_halves = held.tile([P, 2, N], F32, name="b_squared_halves")
+        b_squared_sum = held.tile([P, N], F32, name="b_squared_sum")
+        add_components(b_squared_sum[:], b_squared, b_squared_halves)
+        r = held.tile([P, R, N], F32, name="r")
+        nc.scalar.activation(r[:], b[:], FN.Sqrt)
+        diagonal = held.tile([P, R, N], F32, name="diagonal")
+        nc.scalar.activation(diagonal[:], b_squared[:], FN.Sqrt, bias=1.0)
+        e = held.tile([P, R, N], F32, name="e")
+        nc.vector.tensor_tensor(e[:], diagonal[:], b[:], ALU.subtract)
+
+        weights = [held.tile([P, S], BF16, name=f"weights{m}") for m in range(E)]
+        for m in (1, 2, 3, 4, 0):
+            nc.scalar.activation(weights[m][:], table[m][:], FN.Copy, scale=-1.0 if m == 0 else 1.0)
+
+        s = held.tile([P, R, N], F32, name="s")
+        for k in (1, 2, 3, 4):
+            for m in range(R):
+                q_index, sign = ROTATION[k][m]
+                if k == 1:
+                    nc.vector.tensor_tensor(s[:, m, :], table[k][:].indirect(offsets[:]), q[:, q_index, :], ALU.mult)
+                else:
+                    term = terms.tile([P, N], F32, name="term")
+                    nc.vector.tensor_tensor(term[:], table[k][:].indirect(offsets[:]), q[:, q_index, :], ALU.mult)
+                    nc.vector.tensor_tensor(s[:, m, :], s[:, m, :], term[:], ALU.add if sign > 0 else ALU.subtract)
+
+        time_b = held.tile([P, R, N], F32, name="time_b")
+        for a in range(R):
+            nc.vector.tensor_tensor(time_b[:, a, :], table[0][:].indirect(offsets[:]), b[:, a, :], ALU.mult)
+        time_b_squared = held.tile([P, N], F32, name="time_b_squared")
+        nc.vector.tensor_tensor(time_b_squared[:], table[0][:].indirect(offsets[:]), b_squared_sum[:], ALU.mult)
+
+        b_s = held.tile([P, R, N], F32, name="b_s")
+        nc.vector.tensor_tensor(b_s[:], b[:], s[:], ALU.mult)
+        b_s_halves = held.tile([P, 2, N], F32, name="b_s_halves")
+        b_s_sum = held.tile([P, N], F32, name="b_s_sum")
+        add_components(b_s_sum[:], b_s, b_s_halves)
+        x_time = held.tile([P, N], BF16, name="x_time")
+        nc.vector.tensor_tensor(x_time[:], b_s_sum[:], time_b_squared[:], ALU.add)
+
+        r_s = held.tile([P, R, N], F32, name="r_s")
+        nc.vector.tensor_tensor(r_s[:], r[:], s[:], ALU.mult)
+        r_s_halves = held.tile([P, 2, N], F32, name="r_s_halves")
+        u = held.tile([P, N], F32, name="u")
+        add_components(u[:], r_s, r_s_halves)
+        r_u = held.tile([P, R, N], F32, name="r_u")
+        nc.vector.tensor_tensor(r_u[:], r[:], u[:].unsqueeze(1).to_broadcast([P, R, N]), ALU.mult)
+        e_s = held.tile([P, R, N], F32, name="e_s")
+        nc.vector.tensor_tensor(e_s[:], e[:], s[:], ALU.mult)
+        nc.vector.tensor_tensor(e_s[:], e_s[:], time_b[:], ALU.add)
+        x_space = held.tile([P, R, N], BF16, name="x_space")
+        nc.vector.tensor_tensor(x_space[:], e_s[:], r_u[:], ALU.add)
+
+        x = [x_time[:]] + [x_space[:, a, :] for a in range(R)]
+        out_banks = out.rearrange("(c h p) j -> c p h j", h=2, p=P)
+        for c in range(S // (2 * P)):
+            bank = banks.tile([P, 2, N], F32, name="bank")
+            for h in range(2):
+                block = 2 * c + h
+                for m in range(E):
+                    nc.tensor.matmul(
+                        bank[:, h, :],
+                        weights[m][:, block * P : (block + 1) * P],
+                        x[m],
+                        start=(m == 0),
+                        stop=(m == E - 1),
+                    )
+            scores = staging.tile([P, 2, N], F32, name="scores")
+            if c % 2 == 0:
+                nc.scalar.activation(scores[:], bank[:], FN.Identity, bias=2.0, scale=2.0 / P)
+            else:
+                nc.vector.tensor_scalar(scores[:], bank[:], 2.0 / P, 2.0, ALU.mult, ALU.add)
+            nc.sync.dma_start(out_banks[c, :, :, :], scores[:])

@@ -30,7 +30,7 @@ def tile_lorentzkg_kernel(tc, ent, rot, boost, offs, out):
         tc.tile_pool(name="held", bufs=1) as held,
         tc.tile_pool(name="terms", bufs=4) as terms,
         tc.tile_pool(name="staging", bufs=4) as staging,
-        tc.psum_pool(name="banks", bufs=4) as banks,
+        tc.psum_pool(name="banks", bufs=1) as banks,
     ):
         offsets = held.tile([P, N // 16], U16, name="offsets")
         nc.sync.dma_start(offsets[:], offs)
@@ -85,44 +85,45 @@ def tile_lorentzkg_kernel(tc, ent, rot, boost, offs, out):
         time_b_squared = held.tile([P, N], F32, name="time_b_squared")
         nc.vector.tensor_tensor(time_b_squared[:], table[0][:].indirect(offsets[:]), b_squared_sum[:], ALU.mult)
 
+        x = [held.tile([P, N], BF16, name=f"x{m}") for m in range(E)]
         b_s = held.tile([P, R, N], F32, name="b_s")
         nc.vector.tensor_tensor(b_s[:], b[:], s[:], ALU.mult)
         b_s_halves = held.tile([P, 2, N], F32, name="b_s_halves")
         b_s_sum = held.tile([P, N], F32, name="b_s_sum")
         add_components(b_s_sum[:], b_s, b_s_halves)
-        x_time = held.tile([P, N], BF16, name="x_time")
-        nc.vector.tensor_tensor(x_time[:], b_s_sum[:], time_b_squared[:], ALU.add)
+        nc.vector.tensor_tensor(x[0][:], b_s_sum[:], time_b_squared[:], ALU.add)
 
         r_s = held.tile([P, R, N], F32, name="r_s")
         nc.vector.tensor_tensor(r_s[:], r[:], s[:], ALU.mult)
         r_s_halves = held.tile([P, 2, N], F32, name="r_s_halves")
         u = held.tile([P, N], F32, name="u")
         add_components(u[:], r_s, r_s_halves)
-        r_u = held.tile([P, R, N], F32, name="r_u")
-        nc.vector.tensor_tensor(r_u[:], r[:], u[:].unsqueeze(1).to_broadcast([P, R, N]), ALU.mult)
         e_s = held.tile([P, R, N], F32, name="e_s")
         nc.vector.tensor_tensor(e_s[:], e[:], s[:], ALU.mult)
         nc.vector.tensor_tensor(e_s[:], e_s[:], time_b[:], ALU.add)
-        x_space = held.tile([P, R, N], BF16, name="x_space")
-        nc.vector.tensor_tensor(x_space[:], e_s[:], r_u[:], ALU.add)
+        for a in range(R):
+            r_u = terms.tile([P, N], F32, name="r_u")
+            nc.vector.tensor_tensor(r_u[:], r[:, a, :], u[:], ALU.mult)
+            nc.vector.tensor_tensor(x[1 + a][:], e_s[:, a, :], r_u[:], ALU.add)
 
-        x = [x_time[:]] + [x_space[:, a, :] for a in range(R)]
+        bank = [banks.tile([P, 2, N], F32, name=f"bank{c}") for c in range(S // (2 * P))]
+        for m in range(E):
+            for c in range(S // (2 * P)):
+                for h in range(2):
+                    block = 2 * c + h
+                    nc.tensor.matmul(
+                        bank[c][:, h, :],
+                        weights[m][:, block * P : (block + 1) * P],
+                        x[m][:],
+                        start=(m == 0 and h == 0),
+                        stop=(m == E - 1 and h == 1),
+                    )
+
         out_banks = out.rearrange("(c h p) j -> c p h j", h=2, p=P)
         for c in range(S // (2 * P)):
-            bank = banks.tile([P, 2, N], F32, name="bank")
-            for h in range(2):
-                block = 2 * c + h
-                for m in range(E):
-                    nc.tensor.matmul(
-                        bank[:, h, :],
-                        weights[m][:, block * P : (block + 1) * P],
-                        x[m],
-                        start=(m == 0),
-                        stop=(m == E - 1),
-                    )
             scores = staging.tile([P, 2, N], F32, name="scores")
             if c % 2 == 0:
-                nc.scalar.activation(scores[:], bank[:], FN.Identity, bias=2.0, scale=2.0 / P)
+                nc.scalar.activation(scores[:], bank[c][:], FN.Identity, bias=2.0, scale=2.0 / P)
             else:
-                nc.vector.tensor_scalar(scores[:], bank[:], 2.0 / P, 2.0, ALU.mult, ALU.add)
+                nc.vector.tensor_scalar(scores[:], bank[c][:], 2.0 / P, 2.0, ALU.mult, ALU.add)
             nc.sync.dma_start(out_banks[c, :, :, :], scores[:])

@@ -1,4 +1,5 @@
 import concourse.mybir as mybir
+from concourse.masks import make_identity
 
 F32 = mybir.dt.float32
 BF16 = mybir.dt.bfloat16
@@ -11,6 +12,7 @@ S = 2048
 N = 256
 E = 5
 R = 4
+BANKS = 8
 
 FLOPS = 2 * E * P * S * N
 
@@ -21,106 +23,122 @@ ROTATION = {
     4: ((3, -1), (2, -1), (1, 1), (0, 1)),
 }
 
-SMALLEST_B = 1e-30
+UNDER_THE_ROOT = 1e-30
 
 
 def tile_lorentzkg_kernel(tc, ent, rot, boost, offs, out):
     nc = tc.nc
     with (
         tc.tile_pool(name="held", bufs=1) as held,
-        tc.tile_pool(name="terms", bufs=4) as terms,
+        tc.tile_pool(name="products", bufs=2) as products,
+        tc.tile_pool(name="terms", bufs=2) as terms,
         tc.tile_pool(name="staging", bufs=4) as staging,
-        tc.psum_pool(name="banks", bufs=1) as banks,
+        tc.psum_pool(name="banks", bufs=BANKS) as banks,
     ):
         offsets = held.tile([P, N // 16], U16, name="offsets")
-        nc.sync.dma_start(offsets[:], offs)
         rot_in = held.tile([P, R, N], F32, name="rot_in")
-        nc.scalar.dma_start(rot_in[:], rot.rearrange("(m p) j -> p m j", p=P))
         boost_in = held.tile([P, R, N], F32, name="boost_in")
-        nc.scalar.dma_start(boost_in[:], boost.rearrange("(m p) j -> p m j", p=P))
         table = [held.tile([P, S], F32, name=f"table{m}") for m in range(E)]
-        for m in (1, 2, 3, 4, 0):
+        nc.sync.dma_start(offsets[:], offs)
+        nc.sync.dma_start(rot_in[:], rot.rearrange("(m p) j -> p m j", p=P))
+        nc.sync.dma_start(table[1][:], ent[P : 2 * P, :])
+        nc.sync.dma_start(boost_in[:], boost.rearrange("(m p) j -> p m j", p=P))
+        for m in (2, 3, 4, 0):
             nc.sync.dma_start(table[m][:], ent[m * P : (m + 1) * P, :])
+
+        identity = held.tile([P, P], F32, name="identity")
+        make_identity(nc, identity[:])
+
+        weights = [table[m][:].bitcast(BF16).rearrange("p (n half) -> p n half", half=2) for m in range(E)]
+
+        plus_q = held.tile([P, R, N], F32, name="plus_q")
+        nc.scalar.activation(plus_q[:], rot_in[:], FN.Gelu)
+        minus_q = held.tile([P, R, N], F32, name="minus_q")
+        nc.scalar.activation(minus_q[:], plus_q[:], FN.Copy, scale=-1.0)
+        signed_q = {1: plus_q, -1: minus_q}
+        sigmoid = held.tile([P, R, N], F32, name="sigmoid")
+        nc.scalar.activation(sigmoid[:], boost_in[:], FN.Sigmoid)
+        b = held.tile([P, R, N], F32, name="b")
+        nc.scalar.activation(b[:], sigmoid[:], FN.Copy, scale=0.25)
+        b_squared = held.tile([P, R, N], F32, name="b_squared")
+        nc.scalar.activation(b_squared[:], sigmoid[:], FN.Square, scale=0.25)
+        r = held.tile([P, R, N], F32, name="r")
+        nc.scalar.activation(r[:], sigmoid[:], FN.Sqrt, bias=UNDER_THE_ROOT, scale=0.25)
+        diagonal = held.tile([P, R, N], F32, name="diagonal")
+        nc.scalar.activation(diagonal[:], b_squared[:], FN.Sqrt, bias=1.0)
+
+        s_bank = [banks.tile([P, 2, N], F32, name=f"s_bank{h}", tag="bank") for h in range(2)]
+        for k in (1, 2, 3, 4):
+            product = products.tile([P, R, N], F32, name="product")
+            for m in range(R):
+                q_index, sign = ROTATION[k][m]
+                nc.vector.tensor_tensor(
+                    product[:, m, :],
+                    table[k][:].indirect(offsets[:]),
+                    signed_q[sign][:, q_index, :],
+                    ALU.mult,
+                )
+            for h in range(2):
+                nc.tensor.matmul(
+                    s_bank[h][:].rearrange("p m j -> p (m j)"),
+                    identity[:],
+                    product[:, 2 * h : 2 * h + 2, :].rearrange("p m j -> p (m j)"),
+                    start=(k == 1),
+                    stop=(k == 4),
+                )
+        s = held.tile([P, R, N], F32, name="s")
+        for h in range(2):
+            nc.scalar.copy(s[:, 2 * h : 2 * h + 2, :], s_bank[h][:])
 
         def add_components(total, parts, halves):
             nc.vector.tensor_tensor(halves[:], parts[:, 0:2, :], parts[:, 2:4, :], ALU.add)
             nc.vector.tensor_tensor(total, halves[:, 0, :], halves[:, 1, :], ALU.add)
 
-        q = held.tile([P, R, N], F32, name="q")
-        nc.scalar.activation(q[:], rot_in[:], FN.Gelu)
-        sigmoid = held.tile([P, R, N], F32, name="sigmoid")
-        nc.scalar.activation(sigmoid[:], boost_in[:], FN.Sigmoid)
-        b = held.tile([P, R, N], F32, name="b")
-        nc.vector.tensor_scalar(b[:], sigmoid[:], 0.25, SMALLEST_B, ALU.mult, ALU.max)
-        b_squared = held.tile([P, R, N], F32, name="b_squared")
-        nc.vector.tensor_tensor(b_squared[:], b[:], b[:], ALU.mult)
+        x = [held.tile([P, N], BF16, name=f"x{m}") for m in range(E)]
         b_squared_halves = held.tile([P, 2, N], F32, name="b_squared_halves")
         b_squared_sum = held.tile([P, N], F32, name="b_squared_sum")
         add_components(b_squared_sum[:], b_squared, b_squared_halves)
-        r = held.tile([P, R, N], F32, name="r")
-        nc.scalar.activation(r[:], b[:], FN.Sqrt)
-        diagonal = held.tile([P, R, N], F32, name="diagonal")
-        nc.scalar.activation(diagonal[:], b_squared[:], FN.Sqrt, bias=1.0)
-        e = held.tile([P, R, N], F32, name="e")
-        nc.vector.tensor_tensor(e[:], diagonal[:], b[:], ALU.subtract)
-
-        weights = [held.tile([P, S], BF16, name=f"weights{m}") for m in range(E)]
-        for m in (1, 2, 3, 4, 0):
-            nc.scalar.activation(weights[m][:], table[m][:], FN.Copy, scale=-1.0 if m == 0 else 1.0)
-
-        s = held.tile([P, R, N], F32, name="s")
-        for k in (1, 2, 3, 4):
-            for m in range(R):
-                q_index, sign = ROTATION[k][m]
-                if k == 1:
-                    nc.vector.tensor_tensor(s[:, m, :], table[k][:].indirect(offsets[:]), q[:, q_index, :], ALU.mult)
-                else:
-                    term = terms.tile([P, N], F32, name="term")
-                    nc.vector.tensor_tensor(term[:], table[k][:].indirect(offsets[:]), q[:, q_index, :], ALU.mult)
-                    nc.vector.tensor_tensor(s[:, m, :], s[:, m, :], term[:], ALU.add if sign > 0 else ALU.subtract)
-
-        time_b = held.tile([P, R, N], F32, name="time_b")
-        for a in range(R):
-            nc.vector.tensor_tensor(time_b[:, a, :], table[0][:].indirect(offsets[:]), b[:, a, :], ALU.mult)
         time_b_squared = held.tile([P, N], F32, name="time_b_squared")
         nc.vector.tensor_tensor(time_b_squared[:], table[0][:].indirect(offsets[:]), b_squared_sum[:], ALU.mult)
-
-        x = [held.tile([P, N], BF16, name=f"x{m}") for m in range(E)]
         b_s = held.tile([P, R, N], F32, name="b_s")
         nc.vector.tensor_tensor(b_s[:], b[:], s[:], ALU.mult)
         b_s_halves = held.tile([P, 2, N], F32, name="b_s_halves")
         b_s_sum = held.tile([P, N], F32, name="b_s_sum")
         add_components(b_s_sum[:], b_s, b_s_halves)
-        nc.vector.tensor_tensor(x[0][:], b_s_sum[:], time_b_squared[:], ALU.add)
+        nc.vector.scalar_tensor_tensor(x[0][:], b_s_sum[:], -1.0, time_b_squared[:], ALU.mult, ALU.subtract)
 
         r_s = held.tile([P, R, N], F32, name="r_s")
         nc.vector.tensor_tensor(r_s[:], r[:], s[:], ALU.mult)
         r_s_halves = held.tile([P, 2, N], F32, name="r_s_halves")
         u = held.tile([P, N], F32, name="u")
         add_components(u[:], r_s, r_s_halves)
-        e_s = held.tile([P, R, N], F32, name="e_s")
-        nc.vector.tensor_tensor(e_s[:], e[:], s[:], ALU.mult)
-        nc.vector.tensor_tensor(e_s[:], e_s[:], time_b[:], ALU.add)
         for a in range(R):
+            time_b = terms.tile([P, N], F32, name="time_b")
+            nc.vector.tensor_tensor(time_b[:], table[0][:].indirect(offsets[:]), b[:, a, :], ALU.mult)
+            e = terms.tile([P, N], F32, name="e")
+            nc.vector.tensor_tensor(e[:], diagonal[:, a, :], b[:, a, :], ALU.subtract)
+            e_s = terms.tile([P, N], F32, name="e_s")
+            nc.vector.tensor_tensor(e_s[:], e[:], s[:, a, :], ALU.mult)
+            nc.vector.tensor_tensor(e_s[:], e_s[:], time_b[:], ALU.add)
             r_u = terms.tile([P, N], F32, name="r_u")
             nc.vector.tensor_tensor(r_u[:], r[:, a, :], u[:], ALU.mult)
-            nc.vector.tensor_tensor(x[1 + a][:], e_s[:, a, :], r_u[:], ALU.add)
+            nc.vector.tensor_tensor(x[1 + a][:], e_s[:], r_u[:], ALU.add)
 
-        bank = [banks.tile([P, 2, N], F32, name=f"bank{c}") for c in range(S // (2 * P))]
+        bank = [banks.tile([P, 2, N], F32, name=f"bank{c}", tag="bank") for c in range(BANKS)]
         for m in range(E):
-            for c in range(S // (2 * P)):
+            for c in range(BANKS):
                 for h in range(2):
                     block = 2 * c + h
                     nc.tensor.matmul(
                         bank[c][:, h, :],
-                        weights[m][:, block * P : (block + 1) * P],
+                        weights[m][:, block * P : (block + 1) * P, 1],
                         x[m][:],
                         start=(m == 0 and h == 0),
                         stop=(m == E - 1 and h == 1),
                     )
 
         out_banks = out.rearrange("(c h p) j -> c p h j", h=2, p=P)
-        for c in range(S // (2 * P)):
+        for c in range(BANKS):
             scores = staging.tile([P, 2, N], F32, name="scores")
             if c % 2 == 0:
                 nc.scalar.activation(scores[:], bank[c][:], FN.Identity, bias=2.0, scale=2.0 / P)

@@ -13,6 +13,14 @@ N = 256
 E = 5
 R = 4
 BANKS = 8
+BANK = 512
+BLOCKS = S // P
+
+PIECES = 2
+W = N // PIECES
+BLOCKS_PER_BANK = BANK // W
+BANKS_PER_PIECE = BLOCKS // BLOCKS_PER_BANK
+assert PIECES * BANKS_PER_PIECE <= BANKS
 
 FLOPS = 2 * E * P * S * N
 
@@ -67,81 +75,88 @@ def tile_lorentzkg_kernel(tc, ent, rot, boost, offs, out):
         diagonal = held.tile([P, R, N], F32, name="diagonal")
         nc.scalar.activation(diagonal[:], b_squared[:], FN.Sqrt, bias=1.0)
 
-        s_bank = [banks.tile([P, 2, N], F32, name=f"s_bank{h}", tag="bank") for h in range(2)]
-        for k in (1, 2, 3, 4):
+        def rotation_products(k):
             product = products.tile([P, R, N], F32, name="product")
             for m in range(R):
                 q_index, sign = ROTATION[k][m]
                 nc.vector.tensor_tensor(
-                    product[:, m, :],
-                    table[k][:].indirect(offsets[:]),
-                    signed_q[sign][:, q_index, :],
-                    ALU.mult,
+                    product[:, m, :], table[k][:].indirect(offsets[:]), signed_q[sign][:, q_index, :], ALU.mult
                 )
+            return product
+
+        def add_components(total, parts, halves):
+            nc.vector.tensor_tensor(halves[:], parts[:, 0:2, :], parts[:, 2:4, :], ALU.add)
+            nc.vector.tensor_tensor(total, halves[:, 0, :], halves[:, 1, :], ALU.add)
+
+        s_bank = [banks.tile([P, 2, N], F32, name=f"s_bank{h}", tag="bank") for h in range(2)]
+        for k in (1, 2, 3):
+            product = rotation_products(k)
             for h in range(2):
                 nc.tensor.matmul(
                     s_bank[h][:].rearrange("p m j -> p (m j)"),
                     identity[:],
                     product[:, 2 * h : 2 * h + 2, :].rearrange("p m j -> p (m j)"),
                     start=(k == 1),
-                    stop=(k == 4),
+                    stop=(k == 3),
                 )
-        s = held.tile([P, R, N], F32, name="s")
-        for h in range(2):
-            nc.scalar.copy(s[:, 2 * h : 2 * h + 2, :], s_bank[h][:])
-
-        def add_components(total, parts, halves):
-            nc.vector.tensor_tensor(halves[:], parts[:, 0:2, :], parts[:, 2:4, :], ALU.add)
-            nc.vector.tensor_tensor(total, halves[:, 0, :], halves[:, 1, :], ALU.add)
-
-        x = [held.tile([P, N], BF16, name=f"x{m}") for m in range(E)]
+        last_product = rotation_products(4)
         b_squared_halves = held.tile([P, 2, N], F32, name="b_squared_halves")
         b_squared_sum = held.tile([P, N], F32, name="b_squared_sum")
         add_components(b_squared_sum[:], b_squared, b_squared_halves)
-        time_b_squared = held.tile([P, N], F32, name="time_b_squared")
-        nc.vector.tensor_tensor(time_b_squared[:], table[0][:].indirect(offsets[:]), b_squared_sum[:], ALU.mult)
-        b_s = held.tile([P, R, N], F32, name="b_s")
-        nc.vector.tensor_tensor(b_s[:], b[:], s[:], ALU.mult)
-        b_s_halves = held.tile([P, 2, N], F32, name="b_s_halves")
-        b_s_sum = held.tile([P, N], F32, name="b_s_sum")
-        add_components(b_s_sum[:], b_s, b_s_halves)
-        nc.vector.scalar_tensor_tensor(x[0][:], b_s_sum[:], -1.0, time_b_squared[:], ALU.mult, ALU.subtract)
+        s = held.tile([P, R, N], F32, name="s")
+        for h in range(2):
+            pair = slice(2 * h, 2 * h + 2)
+            nc.vector.tensor_tensor(s[:, pair, :], s_bank[h][:], last_product[:, pair, :], ALU.add)
 
-        r_s = held.tile([P, R, N], F32, name="r_s")
-        nc.vector.tensor_tensor(r_s[:], r[:], s[:], ALU.mult)
-        r_s_halves = held.tile([P, 2, N], F32, name="r_s_halves")
-        u = held.tile([P, N], F32, name="u")
-        add_components(u[:], r_s, r_s_halves)
-        for a in range(R):
-            time_b = terms.tile([P, N], F32, name="time_b")
-            nc.vector.tensor_tensor(time_b[:], table[0][:].indirect(offsets[:]), b[:, a, :], ALU.mult)
-            e = terms.tile([P, N], F32, name="e")
-            nc.vector.tensor_tensor(e[:], diagonal[:, a, :], b[:, a, :], ALU.subtract)
-            e_s = terms.tile([P, N], F32, name="e_s")
-            nc.vector.tensor_tensor(e_s[:], e[:], s[:, a, :], ALU.mult)
-            nc.vector.tensor_tensor(e_s[:], e_s[:], time_b[:], ALU.add)
-            r_u = terms.tile([P, N], F32, name="r_u")
-            nc.vector.tensor_tensor(r_u[:], r[:, a, :], u[:], ALU.mult)
-            nc.vector.tensor_tensor(x[1 + a][:], e_s[:], r_u[:], ALU.add)
+        out_banks = out.rearrange("(c i p) j -> c p i j", i=BLOCKS_PER_BANK, p=P)
+        for piece in range(PIECES):
+            cols = slice(piece * W, (piece + 1) * W)
+            time = table[0][:].indirect(offsets[:, piece * W // 16 : (piece + 1) * W // 16])
 
-        bank = [banks.tile([P, 2, N], F32, name=f"bank{c}", tag="bank") for c in range(BANKS)]
-        for m in range(E):
-            for c in range(BANKS):
-                for h in range(2):
-                    block = 2 * c + h
-                    nc.tensor.matmul(
-                        bank[c][:, h, :],
-                        weights[m][:, block * P : (block + 1) * P, 1],
-                        x[m][:],
-                        start=(m == 0 and h == 0),
-                        stop=(m == E - 1 and h == 1),
-                    )
+            x = [held.tile([P, W], BF16, name=f"x{m}_piece{piece}") for m in range(E)]
+            time_b_squared = terms.tile([P, W], F32, name="time_b_squared")
+            nc.vector.tensor_tensor(time_b_squared[:], time, b_squared_sum[:, cols], ALU.mult)
+            b_s = terms.tile([P, R, W], F32, name="b_s")
+            nc.vector.tensor_tensor(b_s[:], b[:, :, cols], s[:, :, cols], ALU.mult)
+            b_s_halves = terms.tile([P, 2, W], F32, name="b_s_halves")
+            b_s_sum = terms.tile([P, W], F32, name="b_s_sum")
+            add_components(b_s_sum[:], b_s, b_s_halves)
+            nc.vector.scalar_tensor_tensor(x[0][:], b_s_sum[:], -1.0, time_b_squared[:], ALU.mult, ALU.subtract)
 
-        out_banks = out.rearrange("(c h p) j -> c p h j", h=2, p=P)
-        for c in range(BANKS):
-            scores = staging.tile([P, 2, N], F32, name="scores")
-            if c % 2 == 0:
-                nc.scalar.activation(scores[:], bank[c][:], FN.Identity, bias=2.0, scale=2.0 / P)
-            else:
-                nc.vector.tensor_scalar(scores[:], bank[c][:], 2.0 / P, 2.0, ALU.mult, ALU.add)
-            nc.sync.dma_start(out_banks[c, :, :, :], scores[:])
+            r_s = terms.tile([P, R, W], F32, name="r_s")
+            nc.vector.tensor_tensor(r_s[:], r[:, :, cols], s[:, :, cols], ALU.mult)
+            r_s_halves = terms.tile([P, 2, W], F32, name="r_s_halves")
+            u = terms.tile([P, W], F32, name="u")
+            add_components(u[:], r_s, r_s_halves)
+            for a in range(R):
+                time_b = terms.tile([P, W], F32, name="time_b")
+                nc.vector.tensor_tensor(time_b[:], time, b[:, a, cols], ALU.mult)
+                e = terms.tile([P, W], F32, name="e")
+                nc.vector.tensor_tensor(e[:], diagonal[:, a, cols], b[:, a, cols], ALU.subtract)
+                r_u = terms.tile([P, W], F32, name="r_u")
+                nc.vector.tensor_tensor(r_u[:], r[:, a, cols], u[:], ALU.mult)
+                e_s = terms.tile([P, W], F32, name="e_s")
+                nc.vector.tensor_tensor(e_s[:], e[:], s[:, a, cols], ALU.mult)
+                nc.vector.tensor_tensor(r_u[:], r_u[:], time_b[:], ALU.add)
+                nc.vector.tensor_tensor(x[1 + a][:], e_s[:], r_u[:], ALU.add)
+
+            bank = [banks.tile([P, BLOCKS_PER_BANK, W], F32, name=f"bank{c}", tag="bank") for c in range(BANKS_PER_PIECE)]
+            for m in range(E):
+                for c in range(BANKS_PER_PIECE):
+                    for i in range(BLOCKS_PER_BANK):
+                        block = c * BLOCKS_PER_BANK + i
+                        nc.tensor.matmul(
+                            bank[c][:, i, :],
+                            weights[m][:, block * P : (block + 1) * P, 1],
+                            x[m][:],
+                            start=(m == 0 and i == 0),
+                            stop=(m == E - 1 and i == BLOCKS_PER_BANK - 1),
+                        )
+
+            for c in range(BANKS_PER_PIECE):
+                scores = staging.tile([P, BLOCKS_PER_BANK, W], F32, name="scores")
+                if piece == PIECES - 1 and c % 2 == 1:
+                    nc.vector.tensor_scalar(scores[:], bank[c][:], 2.0 / P, 2.0, ALU.mult, ALU.add)
+                else:
+                    nc.scalar.activation(scores[:], bank[c][:], FN.Identity, bias=2.0, scale=2.0 / P)
+                nc.sync.dma_start(out_banks[c, :, :, cols], scores[:])

@@ -38,7 +38,7 @@ def tile_lorentzkg_kernel(tc, ent, rot, boost, offs, out):
     nc = tc.nc
     with (
         tc.tile_pool(name="held", bufs=1) as held,
-        tc.tile_pool(name="products", bufs=2) as products,
+        tc.tile_pool(name="products", bufs=3) as products,
         tc.tile_pool(name="terms", bufs=2) as terms,
         tc.tile_pool(name="staging", bufs=4) as staging,
         tc.psum_pool(name="banks", bufs=BANKS) as banks,
@@ -70,88 +70,116 @@ def tile_lorentzkg_kernel(tc, ent, rot, boost, offs, out):
         nc.scalar.activation(b[:], sigmoid[:], FN.Copy, scale=0.25)
         b_squared = held.tile([P, R, N], F32, name="b_squared")
         nc.scalar.activation(b_squared[:], sigmoid[:], FN.Square, scale=0.25)
-        r = held.tile([P, R, N], F32, name="r")
-        nc.scalar.activation(r[:], sigmoid[:], FN.Sqrt, bias=UNDER_THE_ROOT, scale=0.25)
         diagonal = held.tile([P, R, N], F32, name="diagonal")
         nc.scalar.activation(diagonal[:], b_squared[:], FN.Sqrt, bias=1.0)
+        r = held.tile([P, R, N], F32, name="r")
+        nc.scalar.activation(r[:], sigmoid[:], FN.Sqrt, bias=UNDER_THE_ROOT, scale=0.25)
 
-        def rotation_products(k):
+        def add_components(total, parts, halves):
+            nc.vector.tensor_tensor(halves[:], parts[:, 0:2, :], parts[:, 2:4, :], ALU.add)
+            nc.vector.tensor_tensor(total, halves[:, 0, :], halves[:, 1, :], ALU.add)
+
+        def columns(piece):
+            return slice(piece * W, (piece + 1) * W)
+
+        def entries(piece):
+            return offsets[:, piece * W // 16 : (piece + 1) * W // 16]
+
+        s = [banks.tile([P, R, W], F32, name=f"s_piece{piece}", tag="bank") for piece in range(PIECES)]
+
+        def add_to_s(piece, m, product, first, last):
+            nc.tensor.matmul(s[piece][:, m, :], identity[:], product, start=first, stop=last)
+
+        for k in (1, 2, 3):
             product = products.tile([P, R, N], F32, name="product")
             for m in range(R):
                 q_index, sign = ROTATION[k][m]
                 nc.vector.tensor_tensor(
                     product[:, m, :], table[k][:].indirect(offsets[:]), signed_q[sign][:, q_index, :], ALU.mult
                 )
-            return product
+                for piece in range(PIECES):
+                    add_to_s(piece, m, product[:, m, columns(piece)], first=(k == 1 and m == 0), last=False)
 
-        def add_components(total, parts, halves):
-            nc.vector.tensor_tensor(halves[:], parts[:, 0:2, :], parts[:, 2:4, :], ALU.add)
-            nc.vector.tensor_tensor(total, halves[:, 0, :], halves[:, 1, :], ALU.add)
+        last_product = [held.tile([P, R, W], F32, name=f"last_product{piece}") for piece in range(PIECES)]
+        e = [held.tile([P, R, W], F32, name=f"e{piece}") for piece in range(PIECES)]
+        r_s = [held.tile([P, R, W], F32, name=f"r_s{piece}") for piece in range(PIECES)]
+        e_s = [held.tile([P, R, W], F32, name=f"e_s{piece}") for piece in range(PIECES)]
+        b_s = [held.tile([P, R, W], F32, name=f"b_s{piece}") for piece in range(PIECES)]
+        time_b = [held.tile([P, R, W], F32, name=f"time_b{piece}") for piece in range(PIECES)]
+        u = [held.tile([P, W], F32, name=f"u{piece}") for piece in range(PIECES)]
+        x = [[held.tile([P, W], BF16, name=f"x{m}_piece{piece}") for m in range(E)] for piece in range(PIECES)]
 
-        s_bank = [banks.tile([P, 2, N], F32, name=f"s_bank{h}", tag="bank") for h in range(2)]
-        for k in (1, 2, 3):
-            product = rotation_products(k)
-            for h in range(2):
-                nc.tensor.matmul(
-                    s_bank[h][:].rearrange("p m j -> p (m j)"),
-                    identity[:],
-                    product[:, 2 * h : 2 * h + 2, :].rearrange("p m j -> p (m j)"),
-                    start=(k == 1),
-                    stop=(k == 3),
+        def last_component(piece):
+            for m in range(R):
+                q_index, sign = ROTATION[4][m]
+                nc.vector.tensor_tensor(
+                    last_product[piece][:, m, :],
+                    table[4][:].indirect(entries(piece)),
+                    signed_q[sign][:, q_index, columns(piece)],
+                    ALU.mult,
                 )
-        last_product = rotation_products(4)
-        b_squared_halves = held.tile([P, 2, N], F32, name="b_squared_halves")
-        b_squared_sum = held.tile([P, N], F32, name="b_squared_sum")
-        add_components(b_squared_sum[:], b_squared, b_squared_halves)
-        s = held.tile([P, R, N], F32, name="s")
-        for h in range(2):
-            pair = slice(2 * h, 2 * h + 2)
-            nc.vector.tensor_tensor(s[:, pair, :], s_bank[h][:], last_product[:, pair, :], ALU.add)
+                add_to_s(piece, m, last_product[piece][:, m, :], first=False, last=(m == R - 1))
+
+        def time_component(piece):
+            cols = columns(piece)
+            b_squared_halves = terms.tile([P, 2, W], F32, name="b_squared_halves")
+            b_squared_sum = terms.tile([P, W], F32, name="b_squared_sum")
+            add_components(b_squared_sum[:], b_squared[:, :, cols], b_squared_halves)
+            time_b_squared = terms.tile([P, W], F32, name="time_b_squared")
+            nc.vector.tensor_tensor(time_b_squared[:], table[0][:].indirect(entries(piece)), b_squared_sum[:], ALU.mult)
+            nc.vector.tensor_tensor(b_s[piece][:], b[:, :, cols], s[piece][:], ALU.mult)
+            b_s_halves = terms.tile([P, 2, W], F32, name="b_s_halves")
+            b_s_sum = terms.tile([P, W], F32, name="b_s_sum")
+            add_components(b_s_sum[:], b_s[piece], b_s_halves)
+            nc.vector.scalar_tensor_tensor(
+                x[piece][0][:], b_s_sum[:], -1.0, time_b_squared[:], ALU.mult, ALU.subtract
+            )
+
+        def before_the_spatial_components(piece):
+            cols = columns(piece)
+            nc.vector.tensor_tensor(r_s[piece][:], r[:, :, cols], s[piece][:], ALU.mult)
+            r_s_halves = terms.tile([P, 2, W], F32, name="r_s_halves")
+            add_components(u[piece][:], r_s[piece], r_s_halves)
+            nc.vector.tensor_tensor(e[piece][:], diagonal[:, :, cols], b[:, :, cols], ALU.subtract)
+            nc.vector.tensor_tensor(e_s[piece][:], e[piece][:], s[piece][:], ALU.mult)
+
+        def spatial_component(piece, a):
+            cols = columns(piece)
+            nc.vector.tensor_tensor(
+                time_b[piece][:, a, :], table[0][:].indirect(entries(piece)), b[:, a, cols], ALU.mult
+            )
+            r_u = terms.tile([P, W], F32, name="r_u")
+            nc.vector.tensor_tensor(r_u[:], r[:, a, cols], u[piece][:], ALU.mult)
+            nc.vector.tensor_tensor(r_u[:], r_u[:], e_s[piece][:, a, :], ALU.add)
+            nc.vector.tensor_tensor(x[piece][1 + a][:], r_u[:], time_b[piece][:, a, :], ALU.add)
+
+        def score(piece, bank, m, first, last):
+            for c in range(BANKS_PER_PIECE):
+                for i in range(BLOCKS_PER_BANK):
+                    block = c * BLOCKS_PER_BANK + i
+                    nc.tensor.matmul(
+                        bank[c][:, i, :],
+                        weights[m][:, block * P : (block + 1) * P, 1],
+                        x[piece][m][:],
+                        start=(first and i == 0),
+                        stop=(last and i == BLOCKS_PER_BANK - 1),
+                    )
 
         out_banks = out.rearrange("(c i p) j -> c p i j", i=BLOCKS_PER_BANK, p=P)
         for piece in range(PIECES):
-            cols = slice(piece * W, (piece + 1) * W)
-            time = table[0][:].indirect(offsets[:, piece * W // 16 : (piece + 1) * W // 16])
-
-            x = [held.tile([P, W], BF16, name=f"x{m}_piece{piece}") for m in range(E)]
-            time_b_squared = terms.tile([P, W], F32, name="time_b_squared")
-            nc.vector.tensor_tensor(time_b_squared[:], time, b_squared_sum[:, cols], ALU.mult)
-            b_s = terms.tile([P, R, W], F32, name="b_s")
-            nc.vector.tensor_tensor(b_s[:], b[:, :, cols], s[:, :, cols], ALU.mult)
-            b_s_halves = terms.tile([P, 2, W], F32, name="b_s_halves")
-            b_s_sum = terms.tile([P, W], F32, name="b_s_sum")
-            add_components(b_s_sum[:], b_s, b_s_halves)
-            nc.vector.scalar_tensor_tensor(x[0][:], b_s_sum[:], -1.0, time_b_squared[:], ALU.mult, ALU.subtract)
-
-            r_s = terms.tile([P, R, W], F32, name="r_s")
-            nc.vector.tensor_tensor(r_s[:], r[:, :, cols], s[:, :, cols], ALU.mult)
-            r_s_halves = terms.tile([P, 2, W], F32, name="r_s_halves")
-            u = terms.tile([P, W], F32, name="u")
-            add_components(u[:], r_s, r_s_halves)
-            for a in range(R):
-                time_b = terms.tile([P, W], F32, name="time_b")
-                nc.vector.tensor_tensor(time_b[:], time, b[:, a, cols], ALU.mult)
-                e = terms.tile([P, W], F32, name="e")
-                nc.vector.tensor_tensor(e[:], diagonal[:, a, cols], b[:, a, cols], ALU.subtract)
-                r_u = terms.tile([P, W], F32, name="r_u")
-                nc.vector.tensor_tensor(r_u[:], r[:, a, cols], u[:], ALU.mult)
-                e_s = terms.tile([P, W], F32, name="e_s")
-                nc.vector.tensor_tensor(e_s[:], e[:], s[:, a, cols], ALU.mult)
-                nc.vector.tensor_tensor(r_u[:], r_u[:], time_b[:], ALU.add)
-                nc.vector.tensor_tensor(x[1 + a][:], e_s[:], r_u[:], ALU.add)
-
+            time_first = piece == 0
             bank = [banks.tile([P, BLOCKS_PER_BANK, W], F32, name=f"bank{c}", tag="bank") for c in range(BANKS_PER_PIECE)]
-            for m in range(E):
-                for c in range(BANKS_PER_PIECE):
-                    for i in range(BLOCKS_PER_BANK):
-                        block = c * BLOCKS_PER_BANK + i
-                        nc.tensor.matmul(
-                            bank[c][:, i, :],
-                            weights[m][:, block * P : (block + 1) * P, 1],
-                            x[m][:],
-                            start=(m == 0 and i == 0),
-                            stop=(m == E - 1 and i == BLOCKS_PER_BANK - 1),
-                        )
+            last_component(piece)
+            if time_first:
+                time_component(piece)
+                score(piece, bank, 0, first=True, last=False)
+            before_the_spatial_components(piece)
+            for a in range(R):
+                spatial_component(piece, a)
+                score(piece, bank, 1 + a, first=(a == 0 and not time_first), last=(a == R - 1 and time_first))
+            if not time_first:
+                time_component(piece)
+                score(piece, bank, 0, first=False, last=True)
 
             for c in range(BANKS_PER_PIECE):
                 scores = staging.tile([P, BLOCKS_PER_BANK, W], F32, name="scores")
@@ -159,4 +187,4 @@ def tile_lorentzkg_kernel(tc, ent, rot, boost, offs, out):
                     nc.vector.tensor_scalar(scores[:], bank[c][:], 2.0 / P, 2.0, ALU.mult, ALU.add)
                 else:
                     nc.scalar.activation(scores[:], bank[c][:], FN.Identity, bias=2.0, scale=2.0 / P)
-                nc.sync.dma_start(out_banks[c, :, :, cols], scores[:])
+                nc.sync.dma_start(out_banks[c, :, :, columns(piece)], scores[:])

@@ -68,12 +68,12 @@ def tile_lorentzkg_kernel(tc, ent, rot, boost, offs, out):
         nc.scalar.activation(sigmoid[:], boost_in[:], FN.Sigmoid)
         b = held.tile([P, R, N], F32, name="b")
         nc.scalar.activation(b[:], sigmoid[:], FN.Copy, scale=0.25)
+        r = held.tile([P, R, N], F32, name="r")
+        nc.scalar.activation(r[:], sigmoid[:], FN.Sqrt, bias=UNDER_THE_ROOT, scale=0.25)
         b_squared = held.tile([P, R, N], F32, name="b_squared")
         nc.scalar.activation(b_squared[:], sigmoid[:], FN.Square, scale=0.25)
         diagonal = held.tile([P, R, N], F32, name="diagonal")
         nc.scalar.activation(diagonal[:], b_squared[:], FN.Sqrt, bias=1.0)
-        r = held.tile([P, R, N], F32, name="r")
-        nc.scalar.activation(r[:], sigmoid[:], FN.Sqrt, bias=UNDER_THE_ROOT, scale=0.25)
 
         def add_components(total, parts, halves):
             nc.vector.tensor_tensor(halves[:], parts[:, 0:2, :], parts[:, 2:4, :], ALU.add)

@@ -40,6 +40,7 @@ def tile_lorentzkg_kernel(tc, ent, rot, boost, offs, out):
         tc.tile_pool(name="held", bufs=1) as held,
         tc.tile_pool(name="products", bufs=3) as products,
         tc.tile_pool(name="terms", bufs=2) as terms,
+        tc.tile_pool(name="one_ahead", bufs=2) as one_ahead,
         tc.tile_pool(name="staging", bufs=4) as staging,
         tc.psum_pool(name="banks", bufs=BANKS) as banks,
     ):
@@ -105,7 +106,6 @@ def tile_lorentzkg_kernel(tc, ent, rot, boost, offs, out):
         r_s = [held.tile([P, R, W], F32, name=f"r_s{piece}") for piece in range(PIECES)]
         e_s = [held.tile([P, R, W], F32, name=f"e_s{piece}") for piece in range(PIECES)]
         b_s = [held.tile([P, R, W], F32, name=f"b_s{piece}") for piece in range(PIECES)]
-        time_b = [held.tile([P, R, W], F32, name=f"time_b{piece}") for piece in range(PIECES)]
         u = [held.tile([P, W], F32, name=f"u{piece}") for piece in range(PIECES)]
         x = [[held.tile([P, W], BF16, name=f"x{m}_piece{piece}") for m in range(E)] for piece in range(PIECES)]
 
@@ -145,13 +145,12 @@ def tile_lorentzkg_kernel(tc, ent, rot, boost, offs, out):
 
         def spatial_component(piece, a):
             cols = columns(piece)
-            nc.vector.tensor_tensor(
-                time_b[piece][:, a, :], table[0][:].indirect(entries(piece)), b[:, a, cols], ALU.mult
-            )
+            time_b = one_ahead.tile([P, W], F32, name="time_b")
+            nc.vector.tensor_tensor(time_b[:], table[0][:].indirect(entries(piece)), b[:, a, cols], ALU.mult)
             r_u = terms.tile([P, W], F32, name="r_u")
             nc.vector.tensor_tensor(r_u[:], r[:, a, cols], u[piece][:], ALU.mult)
             nc.vector.tensor_tensor(r_u[:], r_u[:], e_s[piece][:, a, :], ALU.add)
-            nc.vector.tensor_tensor(x[piece][1 + a][:], r_u[:], time_b[piece][:, a, :], ALU.add)
+            nc.vector.tensor_tensor(x[piece][1 + a][:], r_u[:], time_b[:], ALU.add)
 
         def score(piece, bank, m, first, last):
             for c in range(BANKS_PER_PIECE):

import concourse.mybir as mybir
from concourse.masks import make_identity

F32 = mybir.dt.float32
BF16 = mybir.dt.bfloat16
U16 = mybir.dt.uint16
ALU = mybir.AluOpType
FN = mybir.ActivationFunctionType

P = 128
S = 2048
N = 256
E = 5
R = 4
BANKS = 8
BANK = 512
BLOCKS = S // P

PIECES = 2
W = N // PIECES
BLOCKS_PER_BANK = BANK // W
BANKS_PER_PIECE = BLOCKS // BLOCKS_PER_BANK
assert PIECES * BANKS_PER_PIECE <= BANKS

FLOPS = 2 * E * P * S * N

ROTATION = {
    1: ((0, 1), (1, 1), (2, 1), (3, 1)),
    2: ((1, -1), (0, 1), (3, -1), (2, 1)),
    3: ((2, -1), (3, 1), (0, 1), (1, -1)),
    4: ((3, -1), (2, -1), (1, 1), (0, 1)),
}

UNDER_THE_ROOT = 1e-30


def tile_lorentzkg_kernel(tc, ent, rot, boost, offs, out):
    nc = tc.nc
    with (
        tc.tile_pool(name="held", bufs=1) as held,
        tc.tile_pool(name="products", bufs=3) as products,
        tc.tile_pool(name="terms", bufs=2) as terms,
        tc.tile_pool(name="one_ahead", bufs=2) as one_ahead,
        tc.tile_pool(name="staging", bufs=4) as staging,
        tc.psum_pool(name="banks", bufs=BANKS) as banks,
    ):
        offsets = held.tile([P, N // 16], U16, name="offsets")
        rot_in = held.tile([P, R, N], F32, name="rot_in")
        boost_in = held.tile([P, R, N], F32, name="boost_in")
        table = [held.tile([P, S], F32, name=f"table{m}") for m in range(E)]
        nc.sync.dma_start(offsets[:], offs)
        nc.sync.dma_start(rot_in[:], rot.rearrange("(m p) j -> p m j", p=P))
        nc.sync.dma_start(table[1][:], ent[P : 2 * P, :])
        nc.sync.dma_start(boost_in[:], boost.rearrange("(m p) j -> p m j", p=P))
        for m in (2, 3, 4, 0):
            nc.sync.dma_start(table[m][:], ent[m * P : (m + 1) * P, :])

        identity = held.tile([P, P], F32, name="identity")
        make_identity(nc, identity[:])

        weights = [table[m][:].bitcast(BF16).rearrange("p (n half) -> p n half", half=2) for m in range(E)]

        plus_q = held.tile([P, R, N], F32, name="plus_q")
        nc.scalar.activation(plus_q[:], rot_in[:], FN.Gelu)
        minus_q = held.tile([P, R, N], F32, name="minus_q")
        nc.scalar.activation(minus_q[:], plus_q[:], FN.Copy, scale=-1.0)
        signed_q = {1: plus_q, -1: minus_q}
        sigmoid = held.tile([P, R, N], F32, name="sigmoid")
        nc.scalar.activation(sigmoid[:], boost_in[:], FN.Sigmoid)
        b = held.tile([P, R, N], F32, name="b")
        nc.scalar.activation(b[:], sigmoid[:], FN.Copy, scale=0.25)
        r = held.tile([P, R, N], F32, name="r")
        nc.scalar.activation(r[:], sigmoid[:], FN.Sqrt, bias=UNDER_THE_ROOT, scale=0.25)
        b_squared = held.tile([P, R, N], F32, name="b_squared")
        nc.scalar.activation(b_squared[:], sigmoid[:], FN.Square, scale=0.25)
        diagonal = held.tile([P, R, N], F32, name="diagonal")
        nc.scalar.activation(diagonal[:], b_squared[:], FN.Sqrt, bias=1.0)

        def add_components(total, parts, halves):
            nc.vector.tensor_tensor(halves[:], parts[:, 0:2, :], parts[:, 2:4, :], ALU.add)
            nc.vector.tensor_tensor(total, halves[:, 0, :], halves[:, 1, :], ALU.add)

        def columns(piece):
            return slice(piece * W, (piece + 1) * W)

        def entries(piece):
            return offsets[:, piece * W // 16 : (piece + 1) * W // 16]

        s = [banks.tile([P, R, W], F32, name=f"s_piece{piece}", tag="bank") for piece in range(PIECES)]

        def add_to_s(piece, m, product, first, last):
            nc.tensor.matmul(s[piece][:, m, :], identity[:], product, start=first, stop=last)

        for k in (1, 2, 3):
            product = products.tile([P, R, N], F32, name="product")
            for m in range(R):
                q_index, sign = ROTATION[k][m]
                nc.vector.tensor_tensor(
                    product[:, m, :], table[k][:].indirect(offsets[:]), signed_q[sign][:, q_index, :], ALU.mult
                )
                for piece in range(PIECES):
                    add_to_s(piece, m, product[:, m, columns(piece)], first=(k == 1 and m == 0), last=False)

        last_product = [held.tile([P, R, W], F32, name=f"last_product{piece}") for piece in range(PIECES)]
        e = [held.tile([P, R, W], F32, name=f"e{piece}") for piece in range(PIECES)]
        r_s = [held.tile([P, R, W], F32, name=f"r_s{piece}") for piece in range(PIECES)]
        e_s = [held.tile([P, R, W], F32, name=f"e_s{piece}") for piece in range(PIECES)]
        b_s = [held.tile([P, R, W], F32, name=f"b_s{piece}") for piece in range(PIECES)]
        u = [held.tile([P, W], F32, name=f"u{piece}") for piece in range(PIECES)]
        x = [[held.tile([P, W], BF16, name=f"x{m}_piece{piece}") for m in range(E)] for piece in range(PIECES)]

        def last_component(piece):
            for m in range(R):
                q_index, sign = ROTATION[4][m]
                nc.vector.tensor_tensor(
                    last_product[piece][:, m, :],
                    table[4][:].indirect(entries(piece)),
                    signed_q[sign][:, q_index, columns(piece)],
                    ALU.mult,
                )
                add_to_s(piece, m, last_product[piece][:, m, :], first=False, last=(m == R - 1))

        def time_component(piece):
            cols = columns(piece)
            b_squared_halves = terms.tile([P, 2, W], F32, name="b_squared_halves")
            b_squared_sum = terms.tile([P, W], F32, name="b_squared_sum")
            add_components(b_squared_sum[:], b_squared[:, :, cols], b_squared_halves)
            time_b_squared = terms.tile([P, W], F32, name="time_b_squared")
            nc.vector.tensor_tensor(time_b_squared[:], table[0][:].indirect(entries(piece)), b_squared_sum[:], ALU.mult)
            nc.vector.tensor_tensor(b_s[piece][:], b[:, :, cols], s[piece][:], ALU.mult)
            b_s_halves = terms.tile([P, 2, W], F32, name="b_s_halves")
            b_s_sum = terms.tile([P, W], F32, name="b_s_sum")
            add_components(b_s_sum[:], b_s[piece], b_s_halves)
            nc.vector.scalar_tensor_tensor(
                x[piece][0][:], b_s_sum[:], -1.0, time_b_squared[:], ALU.mult, ALU.subtract
            )

        def before_the_spatial_components(piece):
            cols = columns(piece)
            nc.vector.tensor_tensor(r_s[piece][:], r[:, :, cols], s[piece][:], ALU.mult)
            r_s_halves = terms.tile([P, 2, W], F32, name="r_s_halves")
            add_components(u[piece][:], r_s[piece], r_s_halves)
            nc.vector.tensor_tensor(e[piece][:], diagonal[:, :, cols], b[:, :, cols], ALU.subtract)
            nc.vector.tensor_tensor(e_s[piece][:], e[piece][:], s[piece][:], ALU.mult)

        def spatial_component(piece, a):
            cols = columns(piece)
            time_b = one_ahead.tile([P, W], F32, name="time_b")
            nc.vector.tensor_tensor(time_b[:], table[0][:].indirect(entries(piece)), b[:, a, cols], ALU.mult)
            r_u = terms.tile([P, W], F32, name="r_u")
            nc.vector.tensor_tensor(r_u[:], r[:, a, cols], u[piece][:], ALU.mult)
            nc.vector.tensor_tensor(r_u[:], r_u[:], e_s[piece][:, a, :], ALU.add)
            nc.vector.tensor_tensor(x[piece][1 + a][:], r_u[:], time_b[:], ALU.add)

        def score(piece, bank, m, first, last):
            for c in range(BANKS_PER_PIECE):
                for i in range(BLOCKS_PER_BANK):
                    block = c * BLOCKS_PER_BANK + i
                    nc.tensor.matmul(
                        bank[c][:, i, :],
                        weights[m][:, block * P : (block + 1) * P, 1],
                        x[piece][m][:],
                        start=(first and i == 0),
                        stop=(last and i == BLOCKS_PER_BANK - 1),
                    )

        out_banks = out.rearrange("(c i p) j -> c p i j", i=BLOCKS_PER_BANK, p=P)
        for piece in range(PIECES):
            time_first = piece == 0
            bank = [banks.tile([P, BLOCKS_PER_BANK, W], F32, name=f"bank{c}", tag="bank") for c in range(BANKS_PER_PIECE)]
            last_component(piece)
            if time_first:
                time_component(piece)
                score(piece, bank, 0, first=True, last=False)
            before_the_spatial_components(piece)
            for a in range(R):
                spatial_component(piece, a)
                score(piece, bank, 1 + a, first=(a == 0 and not time_first), last=(a == R - 1 and time_first))
            if not time_first:
                time_component(piece)
                score(piece, bank, 0, first=False, last=True)

            for c in range(BANKS_PER_PIECE):
                scores = staging.tile([P, BLOCKS_PER_BANK, W], F32, name="scores")
                if piece == PIECES - 1 and c % 2 == 1:
                    nc.vector.tensor_scalar(scores[:], bank[c][:], 2.0 / P, 2.0, ALU.mult, ALU.add)
                else:
                    nc.scalar.activation(scores[:], bank[c][:], FN.Identity, bias=2.0, scale=2.0 / P)
                nc.sync.dma_start(out_banks[c, :, :, columns(piece)], scores[:])
